import numpy as np
import ml_dtypes


def mxq(x, axis, fmt="e4m3"):
    dtype, down = {"e4m3": (ml_dtypes.float8_e4m3fn, 7), "e5m2": (ml_dtypes.float8_e5m2, 14)}[fmt]
    v = np.moveaxis(np.asarray(x, np.float32).astype(ml_dtypes.bfloat16).astype(np.float64), axis, -1)
    blocks = v.reshape(v.shape[:-1] + (-1, 32))
    amax = np.abs(blocks).max(-1, keepdims=True)
    byte = np.maximum(np.where(amax > 0, np.frexp(amax)[1] - 1 + 127, 0) - down, 1)
    scale = np.exp2(byte - 127.0)
    codes = (blocks / scale).astype(np.float32).astype(dtype).astype(np.float64)
    return np.moveaxis((codes * scale).reshape(v.shape), -1, axis)


WIDE = False


def mx_kscale(k):
    if not WIDE:
        return np.ones(k)
    levels = np.array([20, -20, 10, -10, 0])
    if k % 512:
        return np.exp2(np.random.permutation(np.resize(levels, k // 32))).repeat(32)
    a = np.empty((k // 512, 16))
    for p in range(k // 512):
        a[p, :8] = np.random.permutation(np.resize(levels, 8))
        for g in range(8):
            far = levels[np.abs(levels - a[p, g]) >= 10]
            a[p, g + 8] = far[np.random.randint(len(far))]
    return np.exp2(a.ravel()).repeat(32)


BF16 = ml_dtypes.bfloat16


def bf(x):
    return np.asarray(x, np.float32).astype(BF16)


def f64(x):
    return np.asarray(x).astype(np.float64)


M, K, N = 8192, 512, 512
BITS = 8


def setup_inputs():
    u = mx_kscale(N)
    x = np.random.standard_normal((M, K))
    qw = np.random.randint(0, 2 ** BITS, (N, K)) / u[:, None]
    scale = np.random.uniform(0.01, 0.02, 1) / np.sqrt(K)
    zero_point = np.random.uniform(0.375, 0.625, 1) * 2 ** BITS / u.max()
    bias = np.random.standard_normal(N)
    g = np.random.standard_normal((M, N)) * np.exp2(np.random.randint(-12, 1, (M, 1))) * 8.0 * u
    return {"x": bf(x), "qw": bf(qw), "scale": bf(scale), "zero_point": bf(zero_point),
            "bias": bf(bias), "grad_out": bf(g)}


def reference(x, qw, scale, zero_point, bias, grad_out):
    w = (f64(qw) - f64(zero_point)) * f64(scale)
    return mxq(f64(grad_out), 1, "e5m2") @ mxq(w, 0, "e4m3")

@@ -1,0 +1,153 @@
+from contextlib import ExitStack
+
+import concourse.mybir as mybir
+from concourse.masks import make_identity
+
+F32 = mybir.dt.float32
+BF16 = mybir.dt.bfloat16
+U32 = mybir.dt.uint32
+U8 = mybir.dt.uint8
+E4M3X4 = mybir.dt.float8_e4m3fn_x4
+E5M2X4 = mybir.dt.float8_e5m2_x4
+ALU = mybir.AluOpType
+
+P = 128
+M, N, K = 8192, 512, 512
+T = M // P
+GROUP = 4
+N_GROUPS = T // GROUP
+LOAD_STEPS = [4, 4, 8, 16, 16, 16]
+STORE_STEP = 8
+
+FLOPS = 2 * M * N * K
+BYTES = M * N * 2 + N * K * 2 + 4 + M * K * 4
+
+
+def tile_quantizedlinear_t_kernel(tc, x, qw, scale, zero_point, bias, grad_out, out):
+    nc = tc.nc
+    g_view = grad_out.rearrange("(p t) n -> p t n", t=T)
+    o_view = out.rearrange("(p t) k -> p t k", t=T)
+
+    with ExitStack() as ctx:
+        keep = ctx.enter_context(tc.tile_pool(name="keep", bufs=1))
+        work = ctx.enter_context(tc.tile_pool(name="work", bufs=3))
+        psum = ctx.enter_context(tc.psum_pool(name="psum", bufs=1))
+        ctx.enter_context(tc.manual_schedule())
+
+        row0 = keep.tile([P, 32], BF16)
+        ones = keep.tile([P, P], BF16)
+        nc.gpsimd.memset(row0[:], 0.0)
+        nc.vector.memset(ones[:], 1.0)
+        nc.scalar.dma_start(out=row0[0:1, 0:1], in_=zero_point.unsqueeze(0))
+        nc.scalar.dma_start(out=row0[0:1, 16:17], in_=scale.unsqueeze(0))
+
+        qw_raw = keep.tile([P, 4, K], BF16)
+        nc.sync.dma_start(out=qw_raw[:], in_=qw.rearrange("(p j) c -> p j c", j=4))
+
+        g_words = {}
+        t0 = 0
+        for idx, step in enumerate(LOAD_STEPS):
+            g_sb = keep.tile([P, step, N], BF16, name="g%d" % idx)
+            nc.sync.dma_start(out=g_sb[:], in_=g_view[:, t0 : t0 + step, :])
+            gw = g_sb[:].bitcast(F32)
+            for tl in range(step):
+                g_words[t0 + tl] = gw[:, tl, :]
+            t0 += step
+
+        ident = keep.tile([P, P], F32)
+        make_identity(nc, ident[:])
+
+        spread_ps = psum.tile([P, 32], F32, tag="acc0")
+        nc.tensor.matmul(out=spread_ps[:], lhsT=ones[:], rhs=row0[:], start=True, stop=True)
+        spread = keep.tile([P, 32], F32)
+        nc.vector.tensor_copy(out=spread[:], in_=spread_ps[:])
+        w_grouped = keep.tile([P, K, 4], BF16, align_bytes=64)
+        nc.vector.tensor_scalar(
+            out=w_grouped[:],
+            in0=qw_raw[:].rearrange("p t c -> p c t"),
+            scalar1=spread[:, 0:1],
+            scalar2=spread[:, 16:17],
+            op0=ALU.subtract,
+            op1=ALU.mult,
+        )
+        w_codes = keep.tile([P, K], U32, align_bytes=64)
+        w_scales = keep.tile([P, K], U8, align_bytes=64)
+
+        def quantise_w():
+            nc.vector.quantize_mx(
+                out=w_codes[:].bitcast(E4M3X4),
+                scales=w_scales[:],
+                in_=w_grouped[:].rearrange("p c t -> p (c t)"),
+            )
+
+        xts = {}
+        groupeds = {}
+        quantised = {}
+        o_tiles = {}
+
+        def transposes(i):
+            banks = []
+            for h in range(2):
+                xt = psum.tile([P, 2, 2, P], F32, tag="xt%d" % ((2 * i + h) % 4))
+                for j in range(2):
+                    words = g_words[GROUP * i + 2 * h + j]
+                    for u in range(2):
+                        nc.tensor.transpose(xt[:, j, u, :], words[:, u : 2 * P : 2], ident[:])
+                banks.append(xt)
+            xts[i] = banks
+
+        def regroup(i, copy):
+            grouped = work.tile([P, GROUP * N], BF16, tag="grouped", align_bytes=64)
+            gf = grouped[:].bitcast(F32).rearrange("p (j r u) -> p j r u", j=GROUP, u=2)
+            for h in range(2):
+                copy(
+                    out=gf[:, 2 * h : 2 * h + 2, :, :],
+                    in_=xts[i][h][:].rearrange("p j u r -> p j r u"),
+                )
+            groupeds[i] = grouped
+
+        def quantise(i):
+            codes = work.tile([P, GROUP * P], U32, tag="codes", align_bytes=64)
+            scales = work.tile([P, GROUP * P], U8, tag="scales", align_bytes=64)
+            nc.vector.quantize_mx(out=codes[:].bitcast(E5M2X4), scales=scales[:], in_=groupeds[i][:])
+            quantised[i] = (codes, scales)
+
+        def multiply(i):
+            codes, scales = quantised[i]
+            for k in range(GROUP):
+                t = GROUP * i + k
+                s = t // STORE_STEP
+                if t % STORE_STEP == 0:
+                    o_sb = keep.tile([P, STORE_STEP, K], F32, name="o%d" % s)
+                    o_tiles[s] = o_sb
+                acc = psum.tile([P, K], F32, tag="acc%d" % k)
+                nc.tensor.matmul_mx(
+                    out=acc[:],
+                    lhsT=codes[:, P * k : P * (k + 1)].bitcast(E5M2X4),
+                    lhsT_scale=scales[:, P * k : P * (k + 1)],
+                    rhs=w_codes[:].bitcast(E4M3X4),
+                    rhs_scale=w_scales[:],
+                    start=True,
+                    stop=True,
+                )
+                if i == N_GROUPS - 1 and k % 2 == 1:
+                    nc.vector.tensor_copy(out=o_tiles[s][:, t % STORE_STEP, :], in_=acc[:])
+                else:
+                    nc.scalar.copy(out=o_tiles[s][:, t % STORE_STEP, :], in_=acc[:])
+                if t % STORE_STEP == STORE_STEP - 1:
+                    nc.sync.dma_start(
+                        out=o_view[:, STORE_STEP * s : STORE_STEP * (s + 1), :], in_=o_tiles[s][:]
+                    )
+
+        transposes(0)
+        regroup(0, nc.scalar.copy)
+        quantise_w()
+        transposes(1)
+        regroup(1, nc.scalar.copy)
+        for i in range(N_GROUPS):
+            if 1 <= i and i + 1 < N_GROUPS:
+                regroup(i + 1, nc.vector.tensor_copy)
+            quantise(i)
+            if i + 2 < N_GROUPS:
+                transposes(i + 2)
+            multiply(i)

@@ -36,19 +36,20 @@ def tile_quantizedlinear_t_kernel(tc, x, qw, scale, zero_point, bias, grad_out, 
 
         row0 = keep.tile([P, 32], BF16)
         ones = keep.tile([P, P], BF16)
-        nc.gpsimd.memset(row0[:], 0.0)
+        nc.vector.memset(row0[:], 0.0)
         nc.vector.memset(ones[:], 1.0)
-        nc.scalar.dma_start(out=row0[0:1, 0:1], in_=zero_point.unsqueeze(0))
-        nc.scalar.dma_start(out=row0[0:1, 16:17], in_=scale.unsqueeze(0))
 
         qw_raw = keep.tile([P, 4, K], BF16)
-        nc.sync.dma_start(out=qw_raw[:], in_=qw.rearrange("(p j) c -> p j c", j=4))
-
         g_words = {}
         t0 = 0
         for idx, step in enumerate(LOAD_STEPS):
             g_sb = keep.tile([P, step, N], BF16, name="g%d" % idx)
-            nc.sync.dma_start(out=g_sb[:], in_=g_view[:, t0 : t0 + step, :])
+            queue = nc.scalar if idx == 0 else nc.sync
+            queue.dma_start(out=g_sb[:], in_=g_view[:, t0 : t0 + step, :])
+            if idx == 0:
+                nc.sync.dma_start(out=qw_raw[:], in_=qw.rearrange("(p j) c -> p j c", j=4))
+                nc.sync.dma_start(out=row0[0:1, 0:1], in_=zero_point.unsqueeze(0))
+                nc.sync.dma_start(out=row0[0:1, 16:17], in_=scale.unsqueeze(0))
             gw = g_sb[:].bitcast(F32)
             for tl in range(step):
                 g_words[t0 + tl] = gw[:, tl, :]
@@ -57,21 +58,23 @@ def tile_quantizedlinear_t_kernel(tc, x, qw, scale, zero_point, bias, grad_out, 
         ident = keep.tile([P, P], F32)
         make_identity(nc, ident[:])
 
-        spread_ps = psum.tile([P, 32], F32, tag="acc0")
-        nc.tensor.matmul(out=spread_ps[:], lhsT=ones[:], rhs=row0[:], start=True, stop=True)
-        spread = keep.tile([P, 32], F32)
-        nc.vector.tensor_copy(out=spread[:], in_=spread_ps[:])
         w_grouped = keep.tile([P, K, 4], BF16, align_bytes=64)
-        nc.vector.tensor_scalar(
-            out=w_grouped[:],
-            in0=qw_raw[:].rearrange("p t c -> p c t"),
-            scalar1=spread[:, 0:1],
-            scalar2=spread[:, 16:17],
-            op0=ALU.subtract,
-            op1=ALU.mult,
-        )
         w_codes = keep.tile([P, K], U32, align_bytes=64)
         w_scales = keep.tile([P, K], U8, align_bytes=64)
+
+        def dequantise_w():
+            spread_ps = psum.tile([P, 32], F32, tag="acc0")
+            nc.tensor.matmul(out=spread_ps[:], lhsT=ones[:], rhs=row0[:], start=True, stop=True)
+            spread = keep.tile([P, 32], F32)
+            nc.vector.tensor_copy(out=spread[:], in_=spread_ps[:])
+            nc.vector.tensor_scalar(
+                out=w_grouped[:],
+                in0=qw_raw[:].rearrange("p t c -> p c t"),
+                scalar1=spread[:, 0:1],
+                scalar2=spread[:, 16:17],
+                op0=ALU.subtract,
+                op1=ALU.mult,
+            )
 
         def quantise_w():
             nc.vector.quantize_mx(
@@ -140,14 +143,20 @@ def tile_quantizedlinear_t_kernel(tc, x, qw, scale, zero_point, bias, grad_out, 
                     )
 
         transposes(0)
+        dequantise_w()
         regroup(0, nc.scalar.copy)
+        quantise(0)
         quantise_w()
         transposes(1)
         regroup(1, nc.scalar.copy)
         for i in range(N_GROUPS):
             if 1 <= i and i + 1 < N_GROUPS:
                 regroup(i + 1, nc.vector.tensor_copy)
-            quantise(i)
+            if i >= 1:
+                quantise(i)
+            if i == 0:
+                multiply(0)
             if i + 2 < N_GROUPS:
                 transposes(i + 2)
-            multiply(i)
+            if i >= 1:
+                multiply(i)

@@ -18,6 +18,7 @@ GROUP = 4
 N_GROUPS = T // GROUP
 LOAD_STEPS = [4, 4, 8, 16, 16, 16]
 STORE_STEP = 8
+DMA_ALIGN = 512
 
 FLOPS = 2 * M * N * K
 BYTES = M * N * 2 + N * K * 2 + 4 + M * K * 4
@@ -39,11 +40,11 @@ def tile_quantizedlinear_t_kernel(tc, x, qw, scale, zero_point, bias, grad_out, 
         nc.vector.memset(row0[:], 0.0)
         nc.vector.memset(ones[:], 1.0)
 
-        qw_raw = keep.tile([P, 4, K], BF16)
+        qw_raw = keep.tile([P, 4, K], BF16, align_bytes=DMA_ALIGN)
         g_words = {}
         t0 = 0
         for idx, step in enumerate(LOAD_STEPS):
-            g_sb = keep.tile([P, step, N], BF16, name="g%d" % idx)
+            g_sb = keep.tile([P, step, N], BF16, name="g%d" % idx, align_bytes=DMA_ALIGN)
             queue = nc.scalar if idx == 0 else nc.sync
             queue.dma_start(out=g_sb[:], in_=g_view[:, t0 : t0 + step, :])
             if idx == 0:
@@ -121,7 +122,7 @@ def tile_quantizedlinear_t_kernel(tc, x, qw, scale, zero_point, bias, grad_out, 
                 t = GROUP * i + k
                 s = t // STORE_STEP
                 if t % STORE_STEP == 0:
-                    o_sb = keep.tile([P, STORE_STEP, K], F32, name="o%d" % s)
+                    o_sb = keep.tile([P, STORE_STEP, K], F32, name="o%d" % s, align_bytes=DMA_ALIGN)
                     o_tiles[s] = o_sb
                 acc = psum.tile([P, K], F32, tag="acc%d" % k)
                 nc.tensor.matmul_mx(

@@ -16,7 +16,7 @@ M, N, K = 8192, 512, 512
 T = M // P
 GROUP = 4
 N_GROUPS = T // GROUP
-LOAD_STEPS = [4, 4, 8, 16, 16, 16]
+LOAD_STEPS = [4, 4, 8, 16, 32]
 STORE_STEP = 8
 DMA_ALIGN = 512
 
@@ -45,7 +45,7 @@ def tile_quantizedlinear_t_kernel(tc, x, qw, scale, zero_point, bias, grad_out, 
         t0 = 0
         for idx, step in enumerate(LOAD_STEPS):
             g_sb = keep.tile([P, step, N], BF16, name="g%d" % idx, align_bytes=DMA_ALIGN)
-            queue = nc.scalar if idx == 0 else nc.sync
+            queue = nc.scalar if idx < 2 else nc.sync
             queue.dma_start(out=g_sb[:], in_=g_view[:, t0 : t0 + step, :])
             if idx == 0:
                 nc.sync.dma_start(out=qw_raw[:], in_=qw.rearrange("(p j) c -> p j c", j=4))

from contextlib import ExitStack

import concourse.mybir as mybir
from concourse.masks import make_identity

F32 = mybir.dt.float32
BF16 = mybir.dt.bfloat16
U32 = mybir.dt.uint32
U8 = mybir.dt.uint8
E4M3X4 = mybir.dt.float8_e4m3fn_x4
E5M2X4 = mybir.dt.float8_e5m2_x4
ALU = mybir.AluOpType

P = 128
M, N, K = 8192, 512, 512
T = M // P
GROUP = 4
N_GROUPS = T // GROUP
LOAD_STEPS = [4, 4, 8, 16, 32]
STORE_STEP = 8
DMA_ALIGN = 512

FLOPS = 2 * M * N * K
BYTES = M * N * 2 + N * K * 2 + 4 + M * K * 4


def tile_quantizedlinear_t_kernel(tc, x, qw, scale, zero_point, bias, grad_out, out):
    nc = tc.nc
    g_view = grad_out.rearrange("(p t) n -> p t n", t=T)
    o_view = out.rearrange("(p t) k -> p t k", t=T)

    with ExitStack() as ctx:
        keep = ctx.enter_context(tc.tile_pool(name="keep", bufs=1))
        work = ctx.enter_context(tc.tile_pool(name="work", bufs=3))
        psum = ctx.enter_context(tc.psum_pool(name="psum", bufs=1))
        ctx.enter_context(tc.manual_schedule())

        row0 = keep.tile([P, 32], BF16)
        ones = keep.tile([P, P], BF16)
        nc.vector.memset(row0[:], 0.0)
        nc.vector.memset(ones[:], 1.0)

        qw_raw = keep.tile([P, 4, K], BF16, align_bytes=DMA_ALIGN)
        g_words = {}
        t0 = 0
        for idx, step in enumerate(LOAD_STEPS):
            g_sb = keep.tile([P, step, N], BF16, name="g%d" % idx, align_bytes=DMA_ALIGN)
            queue = nc.scalar if idx < 2 else nc.sync
            queue.dma_start(out=g_sb[:], in_=g_view[:, t0 : t0 + step, :])
            if idx == 0:
                nc.sync.dma_start(out=qw_raw[:], in_=qw.rearrange("(p j) c -> p j c", j=4))
                nc.sync.dma_start(out=row0[0:1, 0:1], in_=zero_point.unsqueeze(0))
                nc.sync.dma_start(out=row0[0:1, 16:17], in_=scale.unsqueeze(0))
            gw = g_sb[:].bitcast(F32)
            for tl in range(step):
                g_words[t0 + tl] = gw[:, tl, :]
            t0 += step

        ident = keep.tile([P, P], F32)
        make_identity(nc, ident[:])

        w_grouped = keep.tile([P, K, 4], BF16, align_bytes=64)
        w_codes = keep.tile([P, K], U32, align_bytes=64)
        w_scales = keep.tile([P, K], U8, align_bytes=64)

        def dequantise_w():
            spread_ps = psum.tile([P, 32], F32, tag="acc0")
            nc.tensor.matmul(out=spread_ps[:], lhsT=ones[:], rhs=row0[:], start=True, stop=True)
            spread = keep.tile([P, 32], F32)
            nc.vector.tensor_copy(out=spread[:], in_=spread_ps[:])
            nc.vector.tensor_scalar(
                out=w_grouped[:],
                in0=qw_raw[:].rearrange("p t c -> p c t"),
                scalar1=spread[:, 0:1],
                scalar2=spread[:, 16:17],
                op0=ALU.subtract,
                op1=ALU.mult,
            )

        def quantise_w():
            nc.vector.quantize_mx(
                out=w_codes[:].bitcast(E4M3X4),
                scales=w_scales[:],
                in_=w_grouped[:].rearrange("p c t -> p (c t)"),
            )

        xts = {}
        groupeds = {}
        quantised = {}
        o_tiles = {}

        def transposes(i):
            banks = []
            for h in range(2):
                xt = psum.tile([P, 2, 2, P], F32, tag="xt%d" % ((2 * i + h) % 4))
                for j in range(2):
                    words = g_words[GROUP * i + 2 * h + j]
                    for u in range(2):
                        nc.tensor.transpose(xt[:, j, u, :], words[:, u : 2 * P : 2], ident[:])
                banks.append(xt)
            xts[i] = banks

        def regroup(i, copy):
            grouped = work.tile([P, GROUP * N], BF16, tag="grouped", align_bytes=64)
            gf = grouped[:].bitcast(F32).rearrange("p (j r u) -> p j r u", j=GROUP, u=2)
            for h in range(2):
                copy(
                    out=gf[:, 2 * h : 2 * h + 2, :, :],
                    in_=xts[i][h][:].rearrange("p j u r -> p j r u"),
                )
            groupeds[i] = grouped

        def quantise(i):
            codes = work.tile([P, GROUP * P], U32, tag="codes", align_bytes=64)
            scales = work.tile([P, GROUP * P], U8, tag="scales", align_bytes=64)
            nc.vector.quantize_mx(out=codes[:].bitcast(E5M2X4), scales=scales[:], in_=groupeds[i][:])
            quantised[i] = (codes, scales)

        def multiply(i):
            codes, scales = quantised[i]
            for k in range(GROUP):
                t = GROUP * i + k
                s = t // STORE_STEP
                if t % STORE_STEP == 0:
                    o_sb = keep.tile([P, STORE_STEP, K], F32, name="o%d" % s, align_bytes=DMA_ALIGN)
                    o_tiles[s] = o_sb
                acc = psum.tile([P, K], F32, tag="acc%d" % k)
                nc.tensor.matmul_mx(
                    out=acc[:],
                    lhsT=codes[:, P * k : P * (k + 1)].bitcast(E5M2X4),
                    lhsT_scale=scales[:, P * k : P * (k + 1)],
                    rhs=w_codes[:].bitcast(E4M3X4),
                    rhs_scale=w_scales[:],
                    start=True,
                    stop=True,
                )
                if i == N_GROUPS - 1 and k % 2 == 1:
                    nc.vector.tensor_copy(out=o_tiles[s][:, t % STORE_STEP, :], in_=acc[:])
                else:
                    nc.scalar.copy(out=o_tiles[s][:, t % STORE_STEP, :], in_=acc[:])
                if t % STORE_STEP == STORE_STEP - 1:
                    nc.sync.dma_start(
                        out=o_view[:, STORE_STEP * s : STORE_STEP * (s + 1), :], in_=o_tiles[s][:]
                    )

        transposes(0)
        dequantise_w()
        regroup(0, nc.scalar.copy)
        quantise(0)
        quantise_w()
        transposes(1)
        regroup(1, nc.scalar.copy)
        for i in range(N_GROUPS):
            if 1 <= i and i + 1 < N_GROUPS:
                regroup(i + 1, nc.vector.tensor_copy)
            if i >= 1:
                quantise(i)
            if i == 0:
                multiply(0)
            if i + 2 < N_GROUPS:
                transposes(i + 2)
            if i >= 1:
                multiply(i)
